import numpy as np
import ml_dtypes


def mxq(x, axis, fmt="e4m3"):
    dtype, down = {"e4m3": (ml_dtypes.float8_e4m3fn, 7), "e5m2": (ml_dtypes.float8_e5m2, 14)}[fmt]
    v = np.moveaxis(np.asarray(x, np.float32).astype(ml_dtypes.bfloat16).astype(np.float64), axis, -1)
    blocks = v.reshape(v.shape[:-1] + (-1, 32))
    amax = np.abs(blocks).max(-1, keepdims=True)
    byte = np.maximum(np.where(amax > 0, np.frexp(amax)[1] - 1 + 127, 0) - down, 1)
    scale = np.exp2(byte - 127.0)
    codes = (blocks / scale).astype(np.float32).astype(dtype).astype(np.float64)
    return np.moveaxis((codes * scale).reshape(v.shape), -1, axis)


WIDE = False


def mx_kscale(k):
    if not WIDE:
        return np.ones(k)
    levels = np.array([10, -10, 5, -5, 0])
    a = np.random.permutation(np.resize(levels, k // 512 * 4)).reshape(k // 512, 4)
    idx = np.arange(k)
    return np.exp2(a[idx // 512, idx % 128 // 32])


BF16 = ml_dtypes.bfloat16


def bf(x):
    return np.asarray(x, np.float32).astype(BF16)


def f64(x):
    return np.asarray(x).astype(np.float64)


M, DIN, D = 1024, 256, 1024


def setup_inputs():
    s = mx_kscale(D)
    s = s / s.max()
    r = np.random.standard_normal
    return {"S": bf(r((M, D)) * s),
            "X": bf(r((M, DIN))),
            "Uz": bf(r((DIN, D)) * 0.5 / np.sqrt(DIN)),
            "Ug": bf(r((DIN, D)) * 0.5 / np.sqrt(DIN)),
            "Ur": bf(r((DIN, D)) * 0.5 / np.sqrt(DIN)),
            "Uh": bf(r((DIN, D)) * 0.5 / np.sqrt(DIN)),
            "Wz": bf(r((D, D)) * 0.7 / np.sqrt(D) / s[:, None]),
            "Wg": bf(r((D, D)) * 0.7 / np.sqrt(D) / s[:, None]),
            "Wr": bf(r((D, D)) * 0.7 / np.sqrt(D) / s[:, None]),
            "Wh": bf(r((D, D)) * 1.0 / np.sqrt(D) / s[:, None]),
            "bz": bf(r((1, D)) * 0.3),
            "bg": bf(r((1, D)) * 0.3),
            "br": bf(r((1, D)) * 0.3),
            "bh": bf(r((1, D)) * 0.3)}


def reference(S, X, Uz, Ug, Ur, Uh, Wz, Wg, Wr, Wh, bz, bg, br, bh):
    Sf = f64(S)
    Sq = mxq(Sf, 1, "e4m3")
    Z = np.tanh(f64(X) @ f64(Uz) + (Sq @ mxq(f64(Wz), 0, "e4m3")) + f64(bz))
    G = np.tanh(f64(X) @ f64(Ug) + (Sq @ mxq(f64(Wg), 0, "e4m3")) + f64(bg))
    R = np.tanh(f64(X) @ f64(Ur) + (Sq @ mxq(f64(Wr), 0, "e4m3")) + f64(br))
    SR = Sf * R
    H = np.tanh(f64(X) @ f64(Uh) + (mxq(SR, 1, "e4m3") @ mxq(f64(Wh), 0, "e4m3")) + f64(bh))
    return (1.0 - G) * H + Z * Sf

@@ -1,0 +1,316 @@
+from contextlib import ExitStack
+
+import concourse.mybir as mybir
+from concourse.masks import make_identity
+
+F32 = mybir.dt.float32
+BF16 = mybir.dt.bfloat16
+U32 = mybir.dt.uint32
+U8 = mybir.dt.uint8
+FP8X4 = mybir.dt.float8_e4m3fn_x4
+ACT = mybir.ActivationFunctionType
+ALU = mybir.AluOpType
+
+P = 128
+PACK = 4
+K_PASS = P * PACK
+TOKENS = 1024
+D = 1024
+DIN = 256
+CHUNK = 512
+PASSES = D // K_PASS
+X_PASSES = DIN // P
+CHUNKS = TOKENS // CHUNK
+ROW_TILES = TOKENS // P
+ROWS_PER_CHUNK = CHUNK // P
+D_TILES = D // P
+HALVES = D // K_PASS
+GATES = ("r", "z", "g", "h")
+GROUP = PACK
+TILES_PER_GATE = HALVES * CHUNKS * GROUP
+GROUPS_PER_GATE = HALVES * CHUNKS
+N_TILES = len(GATES) * TILES_PER_GATE
+FIRST_H = GATES.index("h") * TILES_PER_GATE
+QUARTERS = len(GATES) * HALVES * PASSES
+AHEAD = 8
+QUARTERS_AHEAD = 3
+SR_LAG = 2
+TANH_LAG = 2
+FINISH_LAG = TANH_LAG + 1
+OUT_LAG = GROUP + FINISH_LAG + 2
+
+FLOPS = 2 * TOKENS * D * 4 * (D + DIN)
+
+
+def tile_lstmlayer_pa_kernel(tc, S, X, Uz, Ug, Ur, Uh, Wz, Wg, Wr, Wh, bz, bg, br, bh, out):
+    nc = tc.nc
+    u_dram = {"r": Ur, "z": Uz, "g": Ug, "h": Uh}
+    w_dram = {"r": Wr, "z": Wz, "g": Wg, "h": Wh}
+    b_dram = {"r": br, "z": bz, "g": bg, "h": bh}
+
+    with ExitStack() as ctx:
+        ctx.enter_context(tc.manual_schedule())
+        const = ctx.enter_context(tc.tile_pool(name="const", bufs=1))
+        keep = ctx.enter_context(tc.tile_pool(name="keep", bufs=1))
+        u_pool = ctx.enter_context(tc.tile_pool(name="u", bufs=2))
+        w_pool = ctx.enter_context(tc.tile_pool(name="w", bufs=2))
+        raw_pool = ctx.enter_context(tc.tile_pool(name="raw", bufs=3))
+        grouped_pool = ctx.enter_context(tc.tile_pool(name="grouped", bufs=2))
+        pre_pool = ctx.enter_context(tc.tile_pool(name="pre", bufs=AHEAD + FINISH_LAG + 2))
+        psum_xu = ctx.enter_context(tc.psum_pool(name="psum_xu", bufs=3))
+
+        xT = keep.tile([P, X_PASSES, TOKENS], BF16)
+        sT = keep.tile([P, PASSES, TOKENS, PACK], BF16, align_bytes=64)
+        s_codes = keep.tile([P, PASSES, TOKENS], U32, align_bytes=64)
+        s_scales = keep.tile([P, PASSES, TOKENS], U8, align_bytes=64)
+        sr_codes = keep.tile([P, PASSES, TOKENS], U32, align_bytes=64)
+        sr_scales = keep.tile([P, PASSES, TOKENS], U8, align_bytes=64)
+        zs = keep.tile([P, D_TILES, TOKENS], F32)
+        rg_sb = keep.tile([P, D_TILES, TOKENS], F32)
+
+        u_sb = {}
+        raw = {}
+        grouped = {}
+        w_codes = {}
+        w_scales = {}
+        pre = {}
+        sr_tiles = {}
+
+        def copy_out(which, dest, source):
+            if which % 2 == 0:
+                nc.scalar.copy(out=dest, in_=source)
+            else:
+                nc.vector.tensor_copy(out=dest, in_=source)
+
+        def load_u(gate):
+            u_sb[gate] = u_pool.tile([P, X_PASSES, D], BF16, name="u_" + gate, tag="u")
+            nc.sync.dma_start(out=u_sb[gate][:], in_=u_dram[gate].rearrange("(x p) d -> p x d", p=P))
+
+        def load_weight_half(index):
+            gate, half = divmod(index, HALVES)
+            cols = slice(half * K_PASS, (half + 1) * K_PASS)
+            raw[index] = raw_pool.tile([P, PASSES, PACK, K_PASS], BF16, name="raw" + str(index), tag="raw")
+            nc.sync.dma_start(
+                out=raw[index][:].rearrange("p c t d -> p (c t) d"),
+                in_=w_dram[GATES[gate]][:, cols].rearrange("(ct p) d -> p ct d", p=P),
+            )
+
+        def regroup_quarter(quarter):
+            index, c = divmod(quarter, PASSES)
+            gate = GATES[index // HALVES]
+            if quarter % (HALVES * PASSES) == 0:
+                w_codes[gate] = w_pool.tile([P, PASSES, D], U32, name="w_codes_" + gate, tag="w_codes", align_bytes=64)
+                w_scales[gate] = w_pool.tile([P, PASSES, D], U8, name="w_scales_" + gate, tag="w_scales", align_bytes=64)
+            grouped[quarter] = grouped_pool.tile(
+                [P, K_PASS, PACK], BF16, name="grouped" + str(quarter), tag="grouped", align_bytes=64
+            )
+            nc.vector.tensor_copy(
+                out=grouped[quarter][:].rearrange("p (q i) t -> p q t i", i=4),
+                in_=raw[index][:, c, :, :].rearrange("p t (q i) -> p q t i", i=4),
+            )
+            if c == PASSES - 1 and index + 3 < len(GATES) * HALVES:
+                load_weight_half(index + 3)
+
+        def quantise_quarter(quarter):
+            index, c = divmod(quarter, PASSES)
+            gate, half = divmod(index, HALVES)
+            cols = slice(half * K_PASS, (half + 1) * K_PASS)
+            nc.vector.quantize_mx(
+                out=w_codes[GATES[gate]][:, c, cols].bitcast(FP8X4),
+                scales=w_scales[GATES[gate]][:, c, cols],
+                in_=grouped[quarter][:].rearrange("p d t -> p (d t)"),
+            )
+
+        def where(n):
+            gate = GATES[n // TILES_PER_GATE]
+            half, rest = divmod(n % TILES_PER_GATE, CHUNKS * GROUP)
+            chunk, t = divmod(rest, GROUP)
+            return gate, half * PACK + t, slice(chunk * CHUNK, (chunk + 1) * CHUNK)
+
+        def plain_product(n):
+            gate, j, tok = where(n)
+            xu_ps = psum_xu.tile([P, CHUNK], F32)
+            for x in range(X_PASSES):
+                nc.tensor.matmul(
+                    out=xu_ps[:],
+                    lhsT=u_sb[gate][:, x, j * P : (j + 1) * P],
+                    rhs=xT[:, x, tok],
+                    start=(x == 0),
+                    stop=(x == X_PASSES - 1),
+                )
+            pre[n] = pre_pool.tile([P, CHUNK], F32, name="pre" + str(n), tag="pre")
+            nc.scalar.copy(out=pre[n][:], in_=xu_ps[:])
+            following = n // TILES_PER_GATE + 2
+            if n % TILES_PER_GATE == TILES_PER_GATE - 1 and following < len(GATES):
+                load_u(GATES[following])
+
+        def mx_product(n):
+            gate, j, tok = where(n)
+            a_codes, a_scales = (sr_codes, sr_scales) if gate == "h" else (s_codes, s_scales)
+            mx_ps = psum_mx.tile([P, CHUNK], F32)
+            for c in range(PASSES):
+                nc.tensor.matmul_mx(
+                    out=mx_ps[:],
+                    lhsT=w_codes[gate][:, c, j * P : (j + 1) * P].bitcast(FP8X4),
+                    lhsT_scale=w_scales[gate][:, c, j * P : (j + 1) * P],
+                    rhs=a_codes[:, c, tok].bitcast(FP8X4),
+                    rhs_scale=a_scales[:, c, tok],
+                    start=(c == 0),
+                    stop=(c == PASSES - 1),
+                )
+            nc.vector.tensor_tensor(out=pre[n][:], in0=mx_ps[:], in1=pre[n][:], op=ALU.add)
+
+        def activate(n):
+            gate, j, tok = where(n)
+            group, t = divmod(n, GROUP)
+            if gate == "z":
+                dest = zs[:, j, tok]
+            elif gate == "h":
+                dest = pre[n][:]
+            else:
+                dest = rg_sb[:, j, tok]
+            column = GATES.index(gate) * D_TILES + j
+            nc.scalar.activation(
+                out=dest, in_=pre[n][:], func=ACT.Tanh, bias=bias_col[:, column : column + 1], scale=1.0
+            )
+            if gate == "r" and t == GROUP - 1:
+                sr_tiles[group] = sr_pool.tile([P, CHUNK, PACK], BF16, name="sr" + str(group), tag="sr", align_bytes=64)
+                nc.gpsimd.tensor_tensor(
+                    out=sr_tiles[group][:],
+                    in0=rg_sb[:, j + 1 - PACK : j + 1, tok].rearrange("p t m -> p m t"),
+                    in1=sT[:, j // PACK, tok, :],
+                    op=ALU.mult,
+                )
+            if gate == "z":
+                nc.gpsimd.tensor_tensor(out=dest, in0=dest, in1=sT[:, j // PACK, tok, j % PACK], op=ALU.mult)
+
+        def quantise_sr(group):
+            gate, j, tok = where(group * GROUP)
+            nc.vector.quantize_mx(
+                out=sr_codes[:, j // PACK, tok].bitcast(FP8X4),
+                scales=sr_scales[:, j // PACK, tok],
+                in_=sr_tiles[group][:].rearrange("p m t -> p (m t)"),
+            )
+
+        def combine(n):
+            gate, j, tok = where(n)
+            nc.vector.scalar_tensor_tensor(
+                out=pre[n][:], in0=rg_sb[:, j, tok], scalar=1.0, in1=pre[n][:], op0=ALU.subtract, op1=ALU.mult
+            )
+            nc.gpsimd.tensor_tensor(out=zs[:, j, tok], in0=zs[:, j, tok], in1=pre[n][:], op=ALU.subtract)
+
+        def store_rows(group, i):
+            half, chunk = divmod(group, CHUNKS)
+            r = chunk * ROWS_PER_CHUNK + i
+            back_ps = psum_tr.tile([P, PACK, P], F32, tag="tr")
+            for t in range(PACK):
+                nc.tensor.transpose(back_ps[:, t, :], zs[:, half * PACK + t, r * P : (r + 1) * P], ident_f32[:])
+            rows = rows_pool.tile([P, K_PASS], F32)
+            nc.scalar.copy(out=rows[:], in_=back_ps[:].rearrange("p t d -> p (t d)"))
+            nc.sync.dma_start(out=out[r * P : (r + 1) * P, half * K_PASS : (half + 1) * K_PASS], in_=rows[:])
+
+        with tc.tile_pool(name="natural", bufs=1) as natural, tc.psum_pool(name="psum_in", bufs=5) as psum_in:
+            x_sb = natural.tile([P, ROW_TILES, DIN], BF16)
+            s_sb = natural.tile([P, ROW_TILES, D], BF16)
+            s_rows = S.rearrange("(r p) k -> p r k", p=P)
+            nc.sync.dma_start(out=x_sb[:], in_=X.rearrange("(r p) k -> p r k", p=P))
+            load_u("r")
+            nc.sync.dma_start(out=s_sb[:, :ROWS_PER_CHUNK, :], in_=s_rows[:, :ROWS_PER_CHUNK, :])
+            load_weight_half(0)
+            nc.sync.dma_start(out=s_sb[:, ROWS_PER_CHUNK:, :], in_=s_rows[:, ROWS_PER_CHUNK:, :])
+            load_weight_half(1)
+            load_u("z")
+            load_weight_half(2)
+
+            ident_bf16 = const.tile([P, P], BF16)
+            make_identity(nc, ident_bf16[:])
+            ident_f32 = const.tile([P, P], F32)
+            make_identity(nc, ident_f32[:])
+
+            bias_rows = const.tile([P, P], BF16)
+            nc.vector.memset(bias_rows[:], 0.0)
+            for i, gate in enumerate(GATES):
+                nc.scalar.dma_start(
+                    out=bias_rows[i * D_TILES : (i + 1) * D_TILES, :],
+                    in_=b_dram[gate].rearrange("o (j p) -> (o j) p", p=P),
+                )
+
+            warm = const.tile([P, 1], F32)
+            nc.vector.memset(warm[:], 0.0)
+            nc.scalar.activation(out=warm[:], in_=warm[:], func=ACT.Tanh)
+
+            for x in range(X_PASSES):
+                for chunk in range(CHUNKS):
+                    xt_ps = psum_in.tile([P, ROWS_PER_CHUNK, P], BF16, tag="in")
+                    for i in range(ROWS_PER_CHUNK):
+                        r = chunk * ROWS_PER_CHUNK + i
+                        nc.tensor.transpose(xt_ps[:, i, :], x_sb[:, r, x * P : (x + 1) * P], ident_bf16[:])
+                    copy_out(
+                        chunk, xT[:, x, chunk * CHUNK : (chunk + 1) * CHUNK], xt_ps[:].rearrange("p i m -> p (i m)")
+                    )
+
+            def transpose_s(chunk):
+                for c in range(PASSES):
+                    for i in range(ROWS_PER_CHUNK):
+                        r = chunk * ROWS_PER_CHUNK + i
+                        st_ps = psum_in.tile([P, PACK, P], BF16, tag="in")
+                        for t in range(PACK):
+                            k0 = c * K_PASS + t * P
+                            nc.tensor.transpose(st_ps[:, t, :], s_sb[:, r, k0 : k0 + P], ident_bf16[:])
+                        copy_out(i if chunk == 0 else 0, sT[:, c, r * P : (r + 1) * P, :], st_ps[:].rearrange("p t m -> p m t"))
+
+            def quantise_s(chunk):
+                tok = slice(chunk * CHUNK, (chunk + 1) * CHUNK)
+                for c in range(PASSES):
+                    nc.vector.quantize_mx(
+                        out=s_codes[:, c, tok].bitcast(FP8X4),
+                        scales=s_scales[:, c, tok],
+                        in_=sT[:, c, tok, :].rearrange("p m t -> p (m t)"),
+                    )
+
+            for n in range(AHEAD // 2):
+                plain_product(n)
+            transpose_s(0)
+            regroup_quarter(0)
+            quantise_s(0)
+            regroup_quarter(1)
+            quantise_quarter(0)
+            quantise_quarter(1)
+            for n in range(AHEAD // 2, AHEAD):
+                plain_product(n)
+            transpose_s(1)
+            regroup_quarter(2)
+            quantise_s(1)
+            quantise_quarter(2)
+
+            bias_ps = psum_in.tile([P, P], BF16, tag="in")
+            nc.tensor.transpose(bias_ps[:], bias_rows[:], ident_bf16[:])
+            bias_col = const.tile([P, len(GATES) * D_TILES], F32)
+            nc.vector.tensor_copy(out=bias_col[:], in_=bias_ps[:, : len(GATES) * D_TILES])
+
+        psum_mx = ctx.enter_context(tc.psum_pool(name="psum_mx", bufs=3, reuse_waits="tile"))
+        psum_tr = ctx.enter_context(tc.psum_pool(name="psum_tr", bufs=2, reuse_waits="tile"))
+        sr_pool = ctx.enter_context(tc.tile_pool(name="sr", bufs=SR_LAG + 1))
+        rows_pool = ctx.enter_context(tc.tile_pool(name="rows", bufs=4))
+
+        for n in range(N_TILES + OUT_LAG - 1):
+            group, t = divmod(n, GROUP)
+            if n + AHEAD < N_TILES:
+                plain_product(n + AHEAD)
+            if n < N_TILES:
+                mx_product(n)
+            if 0 <= n - TANH_LAG < N_TILES:
+                activate(n - TANH_LAG)
+            if FIRST_H <= n - FINISH_LAG < N_TILES:
+                combine(n - FINISH_LAG)
+            if group + QUARTERS_AHEAD < QUARTERS:
+                if t == 0:
+                    regroup_quarter(group + QUARTERS_AHEAD)
+                if t == 2:
+                    quantise_quarter(group + QUARTERS_AHEAD)
+            if t == TANH_LAG and 0 <= group - 1 - SR_LAG < GROUPS_PER_GATE:
+                quantise_sr(group - 1 - SR_LAG)
+            pair, odd_step = divmod(n - FIRST_H - OUT_LAG, 2)
+            if pair >= 0 and odd_step == 0:
+                for i in range(2):
+                    store_rows(pair // 2, 2 * (pair % 2) + i)

@@ -34,7 +34,7 @@ FIRST_H = GATES.index("h") * TILES_PER_GATE
 QUARTERS = len(GATES) * HALVES * PASSES
 AHEAD = 8
 QUARTERS_AHEAD = 3
-SR_LAG = 2
+SR_LAG = 3
 TANH_LAG = 2
 FINISH_LAG = TANH_LAG + 1
 OUT_LAG = GROUP + FINISH_LAG + 2
@@ -175,12 +175,13 @@ def tile_lstmlayer_pa_kernel(tc, S, X, Uz, Ug, Ur, Uh, Wz, Wg, Wr, Wh, bz, bg, b
             )
             if gate == "r" and t == GROUP - 1:
                 sr_tiles[group] = sr_pool.tile([P, CHUNK, PACK], BF16, name="sr" + str(group), tag="sr", align_bytes=64)
-                nc.gpsimd.tensor_tensor(
-                    out=sr_tiles[group][:],
-                    in0=rg_sb[:, j + 1 - PACK : j + 1, tok].rearrange("p t m -> p m t"),
-                    in1=sT[:, j // PACK, tok, :],
-                    op=ALU.mult,
-                )
+                r_group = rg_sb[:, j + 1 - PACK : j + 1, tok].rearrange("p t m -> p m t")
+                s_group = sT[:, j // PACK, tok, :]
+                for i in range(ROWS_PER_CHUNK):
+                    piece = slice(i * P, (i + 1) * P)
+                    nc.gpsimd.tensor_tensor(
+                        out=sr_tiles[group][:, piece, :], in0=r_group[:, piece, :], in1=s_group[:, piece, :], op=ALU.mult
+                    )
             if gate == "z":
                 nc.gpsimd.tensor_tensor(out=dest, in0=dest, in1=sT[:, j // PACK, tok, j % PACK], op=ALU.mult)
 
@@ -281,7 +282,6 @@ def tile_lstmlayer_pa_kernel(tc, S, X, Uz, Ug, Ur, Uh, Wz, Wg, Wr, Wh, bz, bg, b
             transpose_s(1)
             regroup_quarter(2)
             quantise_s(1)
-            quantise_quarter(2)
 
             bias_ps = psum_in.tile([P, P], BF16, tag="in")
             nc.tensor.transpose(bias_ps[:], bias_rows[:], ident_bf16[:])
@@ -290,7 +290,7 @@ def tile_lstmlayer_pa_kernel(tc, S, X, Uz, Ug, Ur, Uh, Wz, Wg, Wr, Wh, bz, bg, b
 
         psum_mx = ctx.enter_context(tc.psum_pool(name="psum_mx", bufs=3, reuse_waits="tile"))
         psum_tr = ctx.enter_context(tc.psum_pool(name="psum_tr", bufs=2, reuse_waits="tile"))
-        sr_pool = ctx.enter_context(tc.tile_pool(name="sr", bufs=SR_LAG + 1))
+        sr_pool = ctx.enter_context(tc.tile_pool(name="sr", bufs=SR_LAG))
         rows_pool = ctx.enter_context(tc.tile_pool(name="rows", bufs=4))
 
         for n in range(N_TILES + OUT_LAG - 1):
@@ -303,13 +303,13 @@ def tile_lstmlayer_pa_kernel(tc, S, X, Uz, Ug, Ur, Uh, Wz, Wg, Wr, Wh, bz, bg, b
                 activate(n - TANH_LAG)
             if FIRST_H <= n - FINISH_LAG < N_TILES:
                 combine(n - FINISH_LAG)
-            if group + QUARTERS_AHEAD < QUARTERS:
-                if t == 0:
+            if t == 0:
+                if group + QUARTERS_AHEAD < QUARTERS:
                     regroup_quarter(group + QUARTERS_AHEAD)
-                if t == 2:
-                    quantise_quarter(group + QUARTERS_AHEAD)
-            if t == TANH_LAG and 0 <= group - 1 - SR_LAG < GROUPS_PER_GATE:
-                quantise_sr(group - 1 - SR_LAG)
+                if group + QUARTERS_AHEAD - 1 < QUARTERS:
+                    quantise_quarter(group + QUARTERS_AHEAD - 1)
+                if 0 <= group - SR_LAG < GROUPS_PER_GATE:
+                    quantise_sr(group - SR_LAG)
             pair, odd_step = divmod(n - FIRST_H - OUT_LAG, 2)
             if pair >= 0 and odd_step == 0:
                 for i in range(2):

@@ -171,7 +171,11 @@ def tile_lstmlayer_pa_kernel(tc, S, X, Uz, Ug, Ur, Uh, Wz, Wg, Wr, Wh, bz, bg, b
                 dest = rg_sb[:, j, tok]
             column = GATES.index(gate) * D_TILES + j
             nc.scalar.activation(
-                out=dest, in_=pre[n][:], func=ACT.Tanh, bias=bias_col[:, column : column + 1], scale=1.0
+                out=dest,
+                in_=pre[n][:],
+                func=ACT.Tanh,
+                bias=bias_col[:, column : column + 1],
+                scale=(-1.0 if gate == "g" else 1.0),
             )
             if gate == "r" and t == GROUP - 1:
                 sr_tiles[group] = sr_pool.tile([P, CHUNK, PACK], BF16, name="sr" + str(group), tag="sr", align_bytes=64)
@@ -196,16 +200,21 @@ def tile_lstmlayer_pa_kernel(tc, S, X, Uz, Ug, Ur, Uh, Wz, Wg, Wr, Wh, bz, bg, b
         def combine(n):
             gate, j, tok = where(n)
             nc.vector.scalar_tensor_tensor(
-                out=pre[n][:], in0=rg_sb[:, j, tok], scalar=1.0, in1=pre[n][:], op0=ALU.subtract, op1=ALU.mult
+                out=rg_sb[:, j, tok], in0=rg_sb[:, j, tok], scalar=1.0, in1=pre[n][:], op0=ALU.add, op1=ALU.mult
             )
-            nc.gpsimd.tensor_tensor(out=zs[:, j, tok], in0=zs[:, j, tok], in1=pre[n][:], op=ALU.subtract)
 
         def store_rows(group, i):
             half, chunk = divmod(group, CHUNKS)
             r = chunk * ROWS_PER_CHUNK + i
             back_ps = psum_tr.tile([P, PACK, P], F32, tag="tr")
             for t in range(PACK):
-                nc.tensor.transpose(back_ps[:, t, :], zs[:, half * PACK + t, r * P : (r + 1) * P], ident_f32[:])
+                block = (slice(None), half * PACK + t, slice(r * P, (r + 1) * P))
+                nc.tensor.matmul(
+                    out=back_ps[:, t, :], lhsT=zs[block], rhs=ident_f32[:], is_transpose=True, start=True, stop=False
+                )
+                nc.tensor.matmul(
+                    out=back_ps[:, t, :], lhsT=rg_sb[block], rhs=ident_f32[:], is_transpose=True, start=False, stop=True
+                )
             rows = rows_pool.tile([P, K_PASS], F32)
             nc.scalar.copy(out=rows[:], in_=back_ps[:].rearrange("p t d -> p (t d)"))
             nc.sync.dma_start(out=out[r * P : (r + 1) * P, half * K_PASS : (half + 1) * K_PASS], in_=rows[:])
@@ -287,6 +296,8 @@ def tile_lstmlayer_pa_kernel(tc, S, X, Uz, Ug, Ur, Uh, Wz, Wg, Wr, Wh, bz, bg, b
             nc.tensor.transpose(bias_ps[:], bias_rows[:], ident_bf16[:])
             bias_col = const.tile([P, len(GATES) * D_TILES], F32)
             nc.vector.tensor_copy(out=bias_col[:], in_=bias_ps[:, : len(GATES) * D_TILES])
+            g_columns = slice(GATES.index("g") * D_TILES, (GATES.index("g") + 1) * D_TILES)
+            nc.vector.tensor_scalar_mul(out=bias_col[:, g_columns], in0=bias_col[:, g_columns], scalar1=-1.0)
 
         psum_mx = ctx.enter_context(tc.psum_pool(name="psum_mx", bufs=3, reuse_waits="tile"))
         psum_tr = ctx.enter_context(tc.psum_pool(name="psum_tr", bufs=2, reuse_waits="tile"))

@@ -139,7 +139,7 @@ def tile_lstmlayer_pa_kernel(tc, S, X, Uz, Ug, Ur, Uh, Wz, Wg, Wr, Wh, bz, bg, b
                     stop=(x == X_PASSES - 1),
                 )
             pre[n] = pre_pool.tile([P, CHUNK], F32, name="pre" + str(n), tag="pre")
-            nc.scalar.copy(out=pre[n][:], in_=xu_ps[:])
+            copy_out(1 if n % GROUP == 2 else 0, pre[n][:], xu_ps[:])
             following = n // TILES_PER_GATE + 2
             if n % TILES_PER_GATE == TILES_PER_GATE - 1 and following < len(GATES):
                 load_u(GATES[following])

@@ -57,7 +57,6 @@ def tile_lstmlayer_pa_kernel(tc, S, X, Uz, Ug, Ur, Uh, Wz, Wg, Wr, Wh, bz, bg, b
         raw_pool = ctx.enter_context(tc.tile_pool(name="raw", bufs=3))
         grouped_pool = ctx.enter_context(tc.tile_pool(name="grouped", bufs=2))
         pre_pool = ctx.enter_context(tc.tile_pool(name="pre", bufs=AHEAD + FINISH_LAG + 2))
-        psum_xu = ctx.enter_context(tc.psum_pool(name="psum_xu", bufs=3))
 
         xT = keep.tile([P, X_PASSES, TOKENS], BF16)
         sT = keep.tile([P, PASSES, TOKENS, PACK], BF16, align_bytes=64)
@@ -127,9 +126,9 @@ def tile_lstmlayer_pa_kernel(tc, S, X, Uz, Ug, Ur, Uh, Wz, Wg, Wr, Wh, bz, bg, b
             chunk, t = divmod(rest, GROUP)
             return gate, half * PACK + t, slice(chunk * CHUNK, (chunk + 1) * CHUNK)
 
-        def plain_product(n):
+        def plain_product(n, psum):
             gate, j, tok = where(n)
-            xu_ps = psum_xu.tile([P, CHUNK], F32)
+            xu_ps = psum.tile([P, CHUNK], F32, tag="plain")
             for x in range(X_PASSES):
                 nc.tensor.matmul(
                     out=xu_ps[:],
@@ -139,7 +138,7 @@ def tile_lstmlayer_pa_kernel(tc, S, X, Uz, Ug, Ur, Uh, Wz, Wg, Wr, Wh, bz, bg, b
                     stop=(x == X_PASSES - 1),
                 )
             pre[n] = pre_pool.tile([P, CHUNK], F32, name="pre" + str(n), tag="pre")
-            copy_out(1 if n % GROUP == 2 else 0, pre[n][:], xu_ps[:])
+            nc.scalar.copy(out=pre[n][:], in_=xu_ps[:])
             following = n // TILES_PER_GATE + 2
             if n % TILES_PER_GATE == TILES_PER_GATE - 1 and following < len(GATES):
                 load_u(GATES[following])
@@ -158,7 +157,15 @@ def tile_lstmlayer_pa_kernel(tc, S, X, Uz, Ug, Ur, Uh, Wz, Wg, Wr, Wh, bz, bg, b
                     start=(c == 0),
                     stop=(c == PASSES - 1),
                 )
-            nc.vector.tensor_tensor(out=pre[n][:], in0=mx_ps[:], in1=pre[n][:], op=ALU.add)
+            column = GATES.index(gate) * D_TILES + j
+            nc.vector.scalar_tensor_tensor(
+                out=pre[n][:],
+                in0=mx_ps[:],
+                scalar=bias_col[:, column : column + 1],
+                in1=pre[n][:],
+                op0=ALU.add,
+                op1=ALU.add,
+            )
 
         def activate(n):
             gate, j, tok = where(n)
@@ -169,14 +176,7 @@ def tile_lstmlayer_pa_kernel(tc, S, X, Uz, Ug, Ur, Uh, Wz, Wg, Wr, Wh, bz, bg, b
                 dest = pre[n][:]
             else:
                 dest = rg_sb[:, j, tok]
-            column = GATES.index(gate) * D_TILES + j
-            nc.scalar.activation(
-                out=dest,
-                in_=pre[n][:],
-                func=ACT.Tanh,
-                bias=bias_col[:, column : column + 1],
-                scale=(-1.0 if gate == "g" else 1.0),
-            )
+            nc.scalar.activation(out=dest, in_=pre[n][:], func=ACT.Tanh, scale=(-1.0 if gate == "g" else 1.0))
             if gate == "r" and t == GROUP - 1:
                 sr_tiles[group] = sr_pool.tile([P, CHUNK, PACK], BF16, name="sr" + str(group), tag="sr", align_bytes=64)
                 r_group = rg_sb[:, j + 1 - PACK : j + 1, tok].rearrange("p t m -> p m t")
@@ -206,7 +206,7 @@ def tile_lstmlayer_pa_kernel(tc, S, X, Uz, Ug, Ur, Uh, Wz, Wg, Wr, Wh, bz, bg, b
         def store_rows(group, i):
             half, chunk = divmod(group, CHUNKS)
             r = chunk * ROWS_PER_CHUNK + i
-            back_ps = psum_tr.tile([P, PACK, P], F32, tag="tr")
+            back_ps = psum_plain.tile([P, PACK, P], F32, tag="plain")
             for t in range(PACK):
                 block = (slice(None), half * PACK + t, slice(r * P, (r + 1) * P))
                 nc.tensor.matmul(
@@ -219,7 +219,9 @@ def tile_lstmlayer_pa_kernel(tc, S, X, Uz, Ug, Ur, Uh, Wz, Wg, Wr, Wh, bz, bg, b
             nc.scalar.copy(out=rows[:], in_=back_ps[:].rearrange("p t d -> p (t d)"))
             nc.sync.dma_start(out=out[r * P : (r + 1) * P, half * K_PASS : (half + 1) * K_PASS], in_=rows[:])
 
-        with tc.tile_pool(name="natural", bufs=1) as natural, tc.psum_pool(name="psum_in", bufs=5) as psum_in:
+        with tc.tile_pool(name="natural", bufs=1) as natural, tc.psum_pool(
+            name="psum_in", bufs=5
+        ) as psum_in, tc.psum_pool(name="psum_first", bufs=3) as psum_first:
             x_sb = natural.tile([P, ROW_TILES, DIN], BF16)
             s_sb = natural.tile([P, ROW_TILES, D], BF16)
             s_rows = S.rearrange("(r p) k -> p r k", p=P)
@@ -279,7 +281,7 @@ def tile_lstmlayer_pa_kernel(tc, S, X, Uz, Ug, Ur, Uh, Wz, Wg, Wr, Wh, bz, bg, b
                     )
 
             for n in range(AHEAD // 2):
-                plain_product(n)
+                plain_product(n, psum_first)
             transpose_s(0)
             regroup_quarter(0)
             quantise_s(0)
@@ -287,7 +289,7 @@ def tile_lstmlayer_pa_kernel(tc, S, X, Uz, Ug, Ur, Uh, Wz, Wg, Wr, Wh, bz, bg, b
             quantise_quarter(0)
             quantise_quarter(1)
             for n in range(AHEAD // 2, AHEAD):
-                plain_product(n)
+                plain_product(n, psum_first)
             transpose_s(1)
             regroup_quarter(2)
             quantise_s(1)
@@ -296,18 +298,16 @@ def tile_lstmlayer_pa_kernel(tc, S, X, Uz, Ug, Ur, Uh, Wz, Wg, Wr, Wh, bz, bg, b
             nc.tensor.transpose(bias_ps[:], bias_rows[:], ident_bf16[:])
             bias_col = const.tile([P, len(GATES) * D_TILES], F32)
             nc.vector.tensor_copy(out=bias_col[:], in_=bias_ps[:, : len(GATES) * D_TILES])
-            g_columns = slice(GATES.index("g") * D_TILES, (GATES.index("g") + 1) * D_TILES)
-            nc.vector.tensor_scalar_mul(out=bias_col[:, g_columns], in0=bias_col[:, g_columns], scalar1=-1.0)
 
+        psum_plain = ctx.enter_context(tc.psum_pool(name="psum_plain", bufs=5, reuse_waits="tile"))
         psum_mx = ctx.enter_context(tc.psum_pool(name="psum_mx", bufs=3, reuse_waits="tile"))
-        psum_tr = ctx.enter_context(tc.psum_pool(name="psum_tr", bufs=2, reuse_waits="tile"))
         sr_pool = ctx.enter_context(tc.tile_pool(name="sr", bufs=SR_LAG))
         rows_pool = ctx.enter_context(tc.tile_pool(name="rows", bufs=4))
 
         for n in range(N_TILES + OUT_LAG - 1):
             group, t = divmod(n, GROUP)
             if n + AHEAD < N_TILES:
-                plain_product(n + AHEAD)
+                plain_product(n + AHEAD, psum_plain)
             if n < N_TILES:
                 mx_product(n)
             if 0 <= n - TANH_LAG < N_TILES:

from contextlib import ExitStack

import concourse.mybir as mybir
from concourse.masks import make_identity

F32 = mybir.dt.float32
BF16 = mybir.dt.bfloat16
U32 = mybir.dt.uint32
U8 = mybir.dt.uint8
FP8X4 = mybir.dt.float8_e4m3fn_x4
ACT = mybir.ActivationFunctionType
ALU = mybir.AluOpType

P = 128
PACK = 4
K_PASS = P * PACK
TOKENS = 1024
D = 1024
DIN = 256
CHUNK = 512
PASSES = D // K_PASS
X_PASSES = DIN // P
CHUNKS = TOKENS // CHUNK
ROW_TILES = TOKENS // P
ROWS_PER_CHUNK = CHUNK // P
D_TILES = D // P
HALVES = D // K_PASS
GATES = ("r", "z", "g", "h")
GROUP = PACK
TILES_PER_GATE = HALVES * CHUNKS * GROUP
GROUPS_PER_GATE = HALVES * CHUNKS
N_TILES = len(GATES) * TILES_PER_GATE
FIRST_H = GATES.index("h") * TILES_PER_GATE
QUARTERS = len(GATES) * HALVES * PASSES
AHEAD = 8
QUARTERS_AHEAD = 3
SR_LAG = 3
TANH_LAG = 2
FINISH_LAG = TANH_LAG + 1
OUT_LAG = GROUP + FINISH_LAG + 2

FLOPS = 2 * TOKENS * D * 4 * (D + DIN)


def tile_lstmlayer_pa_kernel(tc, S, X, Uz, Ug, Ur, Uh, Wz, Wg, Wr, Wh, bz, bg, br, bh, out):
    nc = tc.nc
    u_dram = {"r": Ur, "z": Uz, "g": Ug, "h": Uh}
    w_dram = {"r": Wr, "z": Wz, "g": Wg, "h": Wh}
    b_dram = {"r": br, "z": bz, "g": bg, "h": bh}

    with ExitStack() as ctx:
        ctx.enter_context(tc.manual_schedule())
        const = ctx.enter_context(tc.tile_pool(name="const", bufs=1))
        keep = ctx.enter_context(tc.tile_pool(name="keep", bufs=1))
        u_pool = ctx.enter_context(tc.tile_pool(name="u", bufs=2))
        w_pool = ctx.enter_context(tc.tile_pool(name="w", bufs=2))
        raw_pool = ctx.enter_context(tc.tile_pool(name="raw", bufs=3))
        grouped_pool = ctx.enter_context(tc.tile_pool(name="grouped", bufs=2))
        pre_pool = ctx.enter_context(tc.tile_pool(name="pre", bufs=AHEAD + FINISH_LAG + 2))

        xT = keep.tile([P, X_PASSES, TOKENS], BF16)
        sT = keep.tile([P, PASSES, TOKENS, PACK], BF16, align_bytes=64)
        s_codes = keep.tile([P, PASSES, TOKENS], U32, align_bytes=64)
        s_scales = keep.tile([P, PASSES, TOKENS], U8, align_bytes=64)
        sr_codes = keep.tile([P, PASSES, TOKENS], U32, align_bytes=64)
        sr_scales = keep.tile([P, PASSES, TOKENS], U8, align_bytes=64)
        zs = keep.tile([P, D_TILES, TOKENS], F32)
        rg_sb = keep.tile([P, D_TILES, TOKENS], F32)

        u_sb = {}
        raw = {}
        grouped = {}
        w_codes = {}
        w_scales = {}
        pre = {}
        sr_tiles = {}

        def copy_out(which, dest, source):
            if which % 2 == 0:
                nc.scalar.copy(out=dest, in_=source)
            else:
                nc.vector.tensor_copy(out=dest, in_=source)

        def load_u(gate):
            u_sb[gate] = u_pool.tile([P, X_PASSES, D], BF16, name="u_" + gate, tag="u")
            nc.sync.dma_start(out=u_sb[gate][:], in_=u_dram[gate].rearrange("(x p) d -> p x d", p=P))

        def load_weight_half(index):
            gate, half = divmod(index, HALVES)
            cols = slice(half * K_PASS, (half + 1) * K_PASS)
            raw[index] = raw_pool.tile([P, PASSES, PACK, K_PASS], BF16, name="raw" + str(index), tag="raw")
            nc.sync.dma_start(
                out=raw[index][:].rearrange("p c t d -> p (c t) d"),
                in_=w_dram[GATES[gate]][:, cols].rearrange("(ct p) d -> p ct d", p=P),
            )

        def regroup_quarter(quarter):
            index, c = divmod(quarter, PASSES)
            gate = GATES[index // HALVES]
            if quarter % (HALVES * PASSES) == 0:
                w_codes[gate] = w_pool.tile([P, PASSES, D], U32, name="w_codes_" + gate, tag="w_codes", align_bytes=64)
                w_scales[gate] = w_pool.tile([P, PASSES, D], U8, name="w_scales_" + gate, tag="w_scales", align_bytes=64)
            grouped[quarter] = grouped_pool.tile(
                [P, K_PASS, PACK], BF16, name="grouped" + str(quarter), tag="grouped", align_bytes=64
            )
            nc.vector.tensor_copy(
                out=grouped[quarter][:].rearrange("p (q i) t -> p q t i", i=4),
                in_=raw[index][:, c, :, :].rearrange("p t (q i) -> p q t i", i=4),
            )
            if c == PASSES - 1 and index + 3 < len(GATES) * HALVES:
                load_weight_half(index + 3)

        def quantise_quarter(quarter):
            index, c = divmod(quarter, PASSES)
            gate, half = divmod(index, HALVES)
            cols = slice(half * K_PASS, (half + 1) * K_PASS)
            nc.vector.quantize_mx(
                out=w_codes[GATES[gate]][:, c, cols].bitcast(FP8X4),
                scales=w_scales[GATES[gate]][:, c, cols],
                in_=grouped[quarter][:].rearrange("p d t -> p (d t)"),
            )

        def where(n):
            gate = GATES[n // TILES_PER_GATE]
            half, rest = divmod(n % TILES_PER_GATE, CHUNKS * GROUP)
            chunk, t = divmod(rest, GROUP)
            return gate, half * PACK + t, slice(chunk * CHUNK, (chunk + 1) * CHUNK)

        def plain_product(n, psum):
            gate, j, tok = where(n)
            xu_ps = psum.tile([P, CHUNK], F32, tag="plain")
            for x in range(X_PASSES):
                nc.tensor.matmul(
                    out=xu_ps[:],
                    lhsT=u_sb[gate][:, x, j * P : (j + 1) * P],
                    rhs=xT[:, x, tok],
                    start=(x == 0),
                    stop=(x == X_PASSES - 1),
                )
            pre[n] = pre_pool.tile([P, CHUNK], F32, name="pre" + str(n), tag="pre")
            nc.scalar.copy(out=pre[n][:], in_=xu_ps[:])
            following = n // TILES_PER_GATE + 2
            if n % TILES_PER_GATE == TILES_PER_GATE - 1 and following < len(GATES):
                load_u(GATES[following])

        def mx_product(n):
            gate, j, tok = where(n)
            a_codes, a_scales = (sr_codes, sr_scales) if gate == "h" else (s_codes, s_scales)
            mx_ps = psum_mx.tile([P, CHUNK], F32)
            for c in range(PASSES):
                nc.tensor.matmul_mx(
                    out=mx_ps[:],
                    lhsT=w_codes[gate][:, c, j * P : (j + 1) * P].bitcast(FP8X4),
                    lhsT_scale=w_scales[gate][:, c, j * P : (j + 1) * P],
                    rhs=a_codes[:, c, tok].bitcast(FP8X4),
                    rhs_scale=a_scales[:, c, tok],
                    start=(c == 0),
                    stop=(c == PASSES - 1),
                )
            column = GATES.index(gate) * D_TILES + j
            nc.vector.scalar_tensor_tensor(
                out=pre[n][:],
                in0=mx_ps[:],
                scalar=bias_col[:, column : column + 1],
                in1=pre[n][:],
                op0=ALU.add,
                op1=ALU.add,
            )

        def activate(n):
            gate, j, tok = where(n)
            group, t = divmod(n, GROUP)
            if gate == "z":
                dest = zs[:, j, tok]
            elif gate == "h":
                dest = pre[n][:]
            else:
                dest = rg_sb[:, j, tok]
            nc.scalar.activation(out=dest, in_=pre[n][:], func=ACT.Tanh, scale=(-1.0 if gate == "g" else 1.0))
            if gate == "r" and t == GROUP - 1:
                sr_tiles[group] = sr_pool.tile([P, CHUNK, PACK], BF16, name="sr" + str(group), tag="sr", align_bytes=64)
                r_group = rg_sb[:, j + 1 - PACK : j + 1, tok].rearrange("p t m -> p m t")
                s_group = sT[:, j // PACK, tok, :]
                for i in range(ROWS_PER_CHUNK):
                    piece = slice(i * P, (i + 1) * P)
                    nc.gpsimd.tensor_tensor(
                        out=sr_tiles[group][:, piece, :], in0=r_group[:, piece, :], in1=s_group[:, piece, :], op=ALU.mult
                    )
            if gate == "z":
                nc.gpsimd.tensor_tensor(out=dest, in0=dest, in1=sT[:, j // PACK, tok, j % PACK], op=ALU.mult)

        def quantise_sr(group):
            gate, j, tok = where(group * GROUP)
            nc.vector.quantize_mx(
                out=sr_codes[:, j // PACK, tok].bitcast(FP8X4),
                scales=sr_scales[:, j // PACK, tok],
                in_=sr_tiles[group][:].rearrange("p m t -> p (m t)"),
            )

        def combine(n):
            gate, j, tok = where(n)
            nc.vector.scalar_tensor_tensor(
                out=rg_sb[:, j, tok], in0=rg_sb[:, j, tok], scalar=1.0, in1=pre[n][:], op0=ALU.add, op1=ALU.mult
            )

        def store_rows(group, i):
            half, chunk = divmod(group, CHUNKS)
            r = chunk * ROWS_PER_CHUNK + i
            back_ps = psum_plain.tile([P, PACK, P], F32, tag="plain")
            for t in range(PACK):
                block = (slice(None), half * PACK + t, slice(r * P, (r + 1) * P))
                nc.tensor.matmul(
                    out=back_ps[:, t, :], lhsT=zs[block], rhs=ident_f32[:], is_transpose=True, start=True, stop=False
                )
                nc.tensor.matmul(
                    out=back_ps[:, t, :], lhsT=rg_sb[block], rhs=ident_f32[:], is_transpose=True, start=False, stop=True
                )
            rows = rows_pool.tile([P, K_PASS], F32)
            nc.scalar.copy(out=rows[:], in_=back_ps[:].rearrange("p t d -> p (t d)"))
            nc.sync.dma_start(out=out[r * P : (r + 1) * P, half * K_PASS : (half + 1) * K_PASS], in_=rows[:])

        with tc.tile_pool(name="natural", bufs=1) as natural, tc.psum_pool(
            name="psum_in", bufs=5
        ) as psum_in, tc.psum_pool(name="psum_first", bufs=3) as psum_first:
            x_sb = natural.tile([P, ROW_TILES, DIN], BF16)
            s_sb = natural.tile([P, ROW_TILES, D], BF16)
            s_rows = S.rearrange("(r p) k -> p r k", p=P)
            nc.sync.dma_start(out=x_sb[:], in_=X.rearrange("(r p) k -> p r k", p=P))
            load_u("r")
            nc.sync.dma_start(out=s_sb[:, :ROWS_PER_CHUNK, :], in_=s_rows[:, :ROWS_PER_CHUNK, :])
            load_weight_half(0)
            nc.sync.dma_start(out=s_sb[:, ROWS_PER_CHUNK:, :], in_=s_rows[:, ROWS_PER_CHUNK:, :])
            load_weight_half(1)
            load_u("z")
            load_weight_half(2)

            ident_bf16 = const.tile([P, P], BF16)
            make_identity(nc, ident_bf16[:])
            ident_f32 = const.tile([P, P], F32)
            make_identity(nc, ident_f32[:])

            bias_rows = const.tile([P, P], BF16)
            nc.vector.memset(bias_rows[:], 0.0)
            for i, gate in enumerate(GATES):
                nc.scalar.dma_start(
                    out=bias_rows[i * D_TILES : (i + 1) * D_TILES, :],
                    in_=b_dram[gate].rearrange("o (j p) -> (o j) p", p=P),
                )

            warm = const.tile([P, 1], F32)
            nc.vector.memset(warm[:], 0.0)
            nc.scalar.activation(out=warm[:], in_=warm[:], func=ACT.Tanh)

            for x in range(X_PASSES):
                for chunk in range(CHUNKS):
                    xt_ps = psum_in.tile([P, ROWS_PER_CHUNK, P], BF16, tag="in")
                    for i in range(ROWS_PER_CHUNK):
                        r = chunk * ROWS_PER_CHUNK + i
                        nc.tensor.transpose(xt_ps[:, i, :], x_sb[:, r, x * P : (x + 1) * P], ident_bf16[:])
                    copy_out(
                        chunk, xT[:, x, chunk * CHUNK : (chunk + 1) * CHUNK], xt_ps[:].rearrange("p i m -> p (i m)")
                    )

            def transpose_s(chunk):
                for c in range(PASSES):
                    for i in range(ROWS_PER_CHUNK):
                        r = chunk * ROWS_PER_CHUNK + i
                        st_ps = psum_in.tile([P, PACK, P], BF16, tag="in")
                        for t in range(PACK):
                            k0 = c * K_PASS + t * P
                            nc.tensor.transpose(st_ps[:, t, :], s_sb[:, r, k0 : k0 + P], ident_bf16[:])
                        copy_out(i if chunk == 0 else 0, sT[:, c, r * P : (r + 1) * P, :], st_ps[:].rearrange("p t m -> p m t"))

            def quantise_s(chunk):
                tok = slice(chunk * CHUNK, (chunk + 1) * CHUNK)
                for c in range(PASSES):
                    nc.vector.quantize_mx(
                        out=s_codes[:, c, tok].bitcast(FP8X4),
                        scales=s_scales[:, c, tok],
                        in_=sT[:, c, tok, :].rearrange("p m t -> p (m t)"),
                    )

            for n in range(AHEAD // 2):
                plain_product(n, psum_first)
            transpose_s(0)
            regroup_quarter(0)
            quantise_s(0)
            regroup_quarter(1)
            quantise_quarter(0)
            quantise_quarter(1)
            for n in range(AHEAD // 2, AHEAD):
                plain_product(n, psum_first)
            transpose_s(1)
            regroup_quarter(2)
            quantise_s(1)

            bias_ps = psum_in.tile([P, P], BF16, tag="in")
            nc.tensor.transpose(bias_ps[:], bias_rows[:], ident_bf16[:])
            bias_col = const.tile([P, len(GATES) * D_TILES], F32)
            nc.vector.tensor_copy(out=bias_col[:], in_=bias_ps[:, : len(GATES) * D_TILES])

        psum_plain = ctx.enter_context(tc.psum_pool(name="psum_plain", bufs=5, reuse_waits="tile"))
        psum_mx = ctx.enter_context(tc.psum_pool(name="psum_mx", bufs=3, reuse_waits="tile"))
        sr_pool = ctx.enter_context(tc.tile_pool(name="sr", bufs=SR_LAG))
        rows_pool = ctx.enter_context(tc.tile_pool(name="rows", bufs=4))

        for n in range(N_TILES + OUT_LAG - 1):
            group, t = divmod(n, GROUP)
            if n + AHEAD < N_TILES:
                plain_product(n + AHEAD, psum_plain)
            if n < N_TILES:
                mx_product(n)
            if 0 <= n - TANH_LAG < N_TILES:
                activate(n - TANH_LAG)
            if FIRST_H <= n - FINISH_LAG < N_TILES:
                combine(n - FINISH_LAG)
            if t == 0:
                if group + QUARTERS_AHEAD < QUARTERS:
                    regroup_quarter(group + QUARTERS_AHEAD)
                if group + QUARTERS_AHEAD - 1 < QUARTERS:
                    quantise_quarter(group + QUARTERS_AHEAD - 1)
                if 0 <= group - SR_LAG < GROUPS_PER_GATE:
                    quantise_sr(group - SR_LAG)
            pair, odd_step = divmod(n - FIRST_H - OUT_LAG, 2)
            if pair >= 0 and odd_step == 0:
                for i in range(2):
                    store_rows(pair // 2, 2 * (pair % 2) + i)
